import numpy as np
import ml_dtypes


def mxq(x, axis, fmt="e4m3"):
    dtype, down = {"e4m3": (ml_dtypes.float8_e4m3fn, 7), "e5m2": (ml_dtypes.float8_e5m2, 14)}[fmt]
    v = np.moveaxis(np.asarray(x, np.float32).astype(ml_dtypes.bfloat16).astype(np.float64), axis, -1)
    blocks = v.reshape(v.shape[:-1] + (-1, 32))
    amax = np.abs(blocks).max(-1, keepdims=True)
    byte = np.maximum(np.where(amax > 0, np.frexp(amax)[1] - 1 + 127, 0) - down, 1)
    scale = np.exp2(byte - 127.0)
    codes = (blocks / scale).astype(np.float32).astype(dtype).astype(np.float64)
    return np.moveaxis((codes * scale).reshape(v.shape), -1, axis)


WIDE = False


def mx_kscale(k):
    if not WIDE:
        return np.ones(k)
    levels = np.array([10, -10, 5, -5, 0])
    a = np.random.permutation(np.resize(levels, k // 512 * 4)).reshape(k // 512, 4)
    idx = np.arange(k)
    return np.exp2(a[idx // 512, idx % 128 // 32])


BF16 = ml_dtypes.bfloat16


def bf(x):
    return np.asarray(x, np.float32).astype(BF16)


def f64(x):
    return np.asarray(x).astype(np.float64)


B, P, L, K = 1024, 8, 1024, 128
GAUSS_STD = 10.0
PER = 4 * 32


def setup_inputs():
    s = mx_kscale(L)
    r = float(s.max() / s.min())
    f = np.where((np.arange(L) // 32) % 4 == 0, r, 1.0)
    x = np.random.standard_normal((B, P, L)) * 0.5 * f
    u = np.random.random(K) * (L // PER)
    j = np.floor(u)
    weight = u * PER if r == 1.0 else PER * j + 68.0 + 24.0 * (u - j)
    return {"x": bf(x.reshape(B, P * L)), "weight": bf(weight)}


def reference(x, weight):
    t = np.arange(1, L + 1, dtype=np.float64)
    W = np.exp(-((t[:, None] - f64(weight)[None, :]) ** 2) / (GAUSS_STD ** 2))
    xb = f64(x).reshape(B, P, L)
    out = mxq(xb, 2, "e4m3") @ mxq(W, 0, "e4m3")
    return out.reshape(B, P * K)

@@ -1,0 +1,166 @@
+from contextlib import ExitStack
+
+import concourse.mybir as mybir
+from concourse.masks import make_identity
+
+F32 = mybir.dt.float32
+BF16 = mybir.dt.bfloat16
+U32 = mybir.dt.uint32
+U8 = mybir.dt.uint8
+I32 = mybir.dt.int32
+FP8X4 = mybir.dt.float8_e4m3fn_x4
+ACT = mybir.ActivationFunctionType
+
+P = 128
+B, CH, L, K = 1024, 8, 1024, 128
+FLOPS = 2 * B * CH * L * K
+
+CH_CHUNK = 4
+N_BT = B // P
+HALVES = CH // CH_CHUNK
+N_CHUNK = N_BT * HALVES
+COLS = CH_CHUNK * L
+WORDS = COLS // 2
+PASSES = L // 512
+
+
+def tile_samplinglayer_t_kernel(tc, x, weight, out):
+    nc = tc.nc
+    with ExitStack() as ctx:
+        const = ctx.enter_context(tc.tile_pool(name="const", bufs=1))
+        xpool = ctx.enter_context(tc.tile_pool(name="xpool", bufs=N_CHUNK))
+        gpool = ctx.enter_context(tc.tile_pool(name="gpool", bufs=3))
+        qpool = ctx.enter_context(tc.tile_pool(name="qpool", bufs=3))
+        opool = ctx.enter_context(tc.tile_pool(name="opool", bufs=N_BT))
+        ps_t = ctx.enter_context(tc.psum_pool(name="ps_t", bufs=6))
+        ps_o = ctx.enter_context(tc.psum_pool(name="ps_o", bufs=2))
+        ctx.enter_context(tc.manual_schedule())
+
+        wz = const.tile([P, K], BF16)
+        nc.vector.memset(wz[:], 0.0)
+        nc.sync.dma_start(out=wz[0:1, :], in_=weight.rearrange("(o k) -> o k", o=1))
+        x_tiles = []
+        for c in range(N_CHUNK):
+            bt, h = divmod(c, HALVES)
+            x_sb = xpool.tile([P, COLS], BF16)
+            nc.sync.dma_start(
+                out=x_sb[:], in_=x[bt * P : (bt + 1) * P, h * COLS : (h + 1) * COLS]
+            )
+            x_tiles.append(x_sb)
+
+        ident = const.tile([P, P], F32)
+        make_identity(nc, ident[:])
+        ones = const.tile([P, P], BF16)
+        nc.vector.memset(ones[:], 1.0)
+        tiny = const.tile([P, 1], F32)
+        nc.vector.memset(tiny[:], 0.0)
+        tiny2 = const.tile([P, 1], F32)
+        nc.scalar.activation(out=tiny2[:], in_=tiny[:], func=ACT.Exp)
+        l_int = const.tile([P, 8], I32)
+        nc.gpsimd.iota(
+            l_int[:], pattern=[[512, 2], [256, 2], [1, 2]], base=1, channel_multiplier=2
+        )
+        l_f32 = const.tile([P, 8], F32)
+        nc.vector.tensor_copy(out=l_f32[:], in_=l_int[:])
+
+        wb = ps_o.tile([P, K], F32, tag="ob")
+        nc.tensor.matmul(wb[:], lhsT=ones[:], rhs=wz[:], start=True, stop=True)
+        sq = const.tile([P, 8, K], F32)
+        for j in range(8):
+            nc.scalar.activation(
+                out=sq[:, j, :], in_=wb[:], func=ACT.Square, bias=l_f32[:, j : j + 1], scale=-1.0
+            )
+        w_grouped = const.tile([P, PASSES * K * 4], BF16, align_bytes=64)
+        nc.scalar.activation(
+            out=w_grouped[:].rearrange("q (g k t) -> q g k t", g=PASSES, t=4),
+            in_=sq[:].rearrange("q (g t) k -> q g k t", g=PASSES),
+            func=ACT.Exp,
+            scale=-0.01,
+        )
+        w_codes = const.tile([P, PASSES * K], U32, align_bytes=64)
+        w_scales = const.tile([P, PASSES * K], U8, align_bytes=64)
+        nc.vector.quantize_mx(out=w_codes[:].bitcast(FP8X4), scales=w_scales[:], in_=w_grouped[:])
+
+        state = {}
+
+        def transposes(c):
+            xw = x_tiles[c][:].bitcast(F32)
+            banks = []
+            for p in range(CH_CHUNK):
+                xt = ps_t.tile([P, 4, P], F32)
+                for j in range(4):
+                    col = p * 512 + j * P
+                    nc.tensor.transpose(xt[:, j, :], xw[:, col : col + P], ident[:])
+                banks.append(xt)
+            state[("xt", c)] = banks
+
+        def copy_bank(c, p, engine):
+            grouped = state[("gr", c)]
+            dst = grouped[:].bitcast(F32)[:, p * 512 : (p + 1) * 512].rearrange(
+                "q (g b u) -> q g b u", g=PASSES, u=2
+            )
+            src = state[("xt", c)][p][:].rearrange("q (g u) b -> q g b u", u=2)
+            if engine == "v":
+                nc.vector.tensor_copy(out=dst, in_=src)
+            else:
+                nc.scalar.copy(out=dst, in_=src)
+
+        def quantise(c, half):
+            grouped = state[("gr", c)]
+            codes, scales = state[("q", c)]
+            w = COLS // 2
+            nc.vector.quantize_mx(
+                out=codes[:, half * (w // 4) : (half + 1) * (w // 4)].bitcast(FP8X4),
+                scales=scales[:, half * (w // 4) : (half + 1) * (w // 4)],
+                in_=grouped[:, half * w : (half + 1) * w],
+            )
+
+        def multiply(c):
+            codes, scales = state[("q", c)]
+            ob = ps_o.tile([P, CH_CHUNK * K], F32, tag="ob")
+            for p in range(CH_CHUNK):
+                for g in range(PASSES):
+                    col = (p * PASSES + g) * P
+                    nc.tensor.matmul_mx(
+                        out=ob[:, p * K : (p + 1) * K],
+                        lhsT=codes[:, col : col + P].bitcast(FP8X4),
+                        lhsT_scale=scales[:, col : col + P],
+                        rhs=w_codes[:, g * K : (g + 1) * K].bitcast(FP8X4),
+                        rhs_scale=w_scales[:, g * K : (g + 1) * K],
+                        start=(g == 0),
+                        stop=(g == PASSES - 1),
+                    )
+            state[("ob", c)] = ob
+
+        def result(c):
+            bt, h = divmod(c, HALVES)
+            if h == 0:
+                o_sb = opool.tile([P, CH * K], F32)
+                state[("o", bt)] = o_sb
+            o_sb = state[("o", bt)]
+            dst = o_sb[:, h * CH_CHUNK * K : (h + 1) * CH_CHUNK * K]
+            if c % 2 == 1:
+                nc.vector.tensor_copy(out=dst, in_=state[("ob", c)][:])
+            else:
+                nc.scalar.copy(out=dst, in_=state[("ob", c)][:])
+            if h == HALVES - 1:
+                nc.sync.dma_start(out=out[bt * P : (bt + 1) * P, :], in_=o_sb[:])
+
+        for c in range(N_CHUNK + 1):
+            if c < N_CHUNK:
+                transposes(c)
+                grouped = gpool.tile([P, COLS], BF16, align_bytes=64)
+                state[("gr", c)] = grouped
+                codes = qpool.tile([P, COLS // 4], U32, align_bytes=64)
+                scales = qpool.tile([P, COLS // 4], U8, align_bytes=64)
+                state[("q", c)] = (codes, scales)
+                copy_bank(c, 0, "v")
+                copy_bank(c, 1, "s")
+                copy_bank(c, 2, "s")
+                copy_bank(c, 3, "s")
+                quantise(c, 0)
+            if c >= 1:
+                multiply(c - 1)
+                result(c - 1)
+            if c < N_CHUNK:
+                quantise(c, 1)

@@ -20,15 +20,17 @@ N_BT = B // P
 HALVES = CH // CH_CHUNK
 N_CHUNK = N_BT * HALVES
 COLS = CH_CHUNK * L
-WORDS = COLS // 2
 PASSES = L // 512
+WARM = 3
+FILL = 3
 
 
 def tile_samplinglayer_t_kernel(tc, x, weight, out):
     nc = tc.nc
     with ExitStack() as ctx:
         const = ctx.enter_context(tc.tile_pool(name="const", bufs=1))
-        xpool = ctx.enter_context(tc.tile_pool(name="xpool", bufs=N_CHUNK))
+        fpool = ctx.enter_context(tc.tile_pool(name="fpool", bufs=CH_CHUNK))
+        xpool = ctx.enter_context(tc.tile_pool(name="xpool", bufs=N_CHUNK - 1))
         gpool = ctx.enter_context(tc.tile_pool(name="gpool", bufs=3))
         qpool = ctx.enter_context(tc.tile_pool(name="qpool", bufs=3))
         opool = ctx.enter_context(tc.tile_pool(name="opool", bufs=N_BT))
@@ -39,14 +41,19 @@ def tile_samplinglayer_t_kernel(tc, x, weight, out):
         wz = const.tile([P, K], BF16)
         nc.vector.memset(wz[:], 0.0)
         nc.sync.dma_start(out=wz[0:1, :], in_=weight.rearrange("(o k) -> o k", o=1))
-        x_tiles = []
-        for c in range(N_CHUNK):
+        words = {}
+        for p in range(CH_CHUNK):
+            x_first = fpool.tile([P, L], BF16)
+            nc.sync.dma_start(out=x_first[:], in_=x[0:P, p * L : (p + 1) * L])
+            words[(0, p)] = x_first[:].bitcast(F32)
+        for c in range(1, N_CHUNK):
             bt, h = divmod(c, HALVES)
             x_sb = xpool.tile([P, COLS], BF16)
             nc.sync.dma_start(
                 out=x_sb[:], in_=x[bt * P : (bt + 1) * P, h * COLS : (h + 1) * COLS]
             )
-            x_tiles.append(x_sb)
+            for p in range(CH_CHUNK):
+                words[(c, p)] = x_sb[:].bitcast(F32)[:, p * 512 : (p + 1) * 512]
 
         ident = const.tile([P, P], F32)
         make_identity(nc, ident[:])
@@ -63,8 +70,17 @@ def tile_samplinglayer_t_kernel(tc, x, weight, out):
         l_f32 = const.tile([P, 8], F32)
         nc.vector.tensor_copy(out=l_f32[:], in_=l_int[:])
 
+        idle = ps_o.tile([P, P], F32, tag="ob")
+
+        def fillers(n):
+            for i in range(n):
+                nc.tensor.matmul(idle[:], lhsT=ident[:], rhs=ident[:], start=True, stop=True)
+
+        fillers(WARM)
+
         wb = ps_o.tile([P, K], F32, tag="ob")
         nc.tensor.matmul(wb[:], lhsT=ones[:], rhs=wz[:], start=True, stop=True)
+        fillers(1)
         sq = const.tile([P, 8, K], F32)
         for j in range(8):
             nc.scalar.activation(
@@ -79,20 +95,21 @@ def tile_samplinglayer_t_kernel(tc, x, weight, out):
         )
         w_codes = const.tile([P, PASSES * K], U32, align_bytes=64)
         w_scales = const.tile([P, PASSES * K], U8, align_bytes=64)
-        nc.vector.quantize_mx(out=w_codes[:].bitcast(FP8X4), scales=w_scales[:], in_=w_grouped[:])
 
         state = {}
 
         def transposes(c):
-            xw = x_tiles[c][:].bitcast(F32)
             banks = []
             for p in range(CH_CHUNK):
                 xt = ps_t.tile([P, 4, P], F32)
                 for j in range(4):
-                    col = p * 512 + j * P
-                    nc.tensor.transpose(xt[:, j, :], xw[:, col : col + P], ident[:])
+                    nc.tensor.transpose(xt[:, j, :], words[(c, p)][:, j * P : (j + 1) * P], ident[:])
                 banks.append(xt)
+                if c == 0:
+                    fillers(1)
             state[("xt", c)] = banks
+            if c < 2:
+                fillers(FILL)
 
         def copy_bank(c, p, engine):
             grouped = state[("gr", c)]
@@ -105,15 +122,16 @@ def tile_samplinglayer_t_kernel(tc, x, weight, out):
             else:
                 nc.scalar.copy(out=dst, in_=src)
 
-        def quantise(c, half):
+        def quantise(c, parts):
             grouped = state[("gr", c)]
             codes, scales = state[("q", c)]
-            w = COLS // 2
-            nc.vector.quantize_mx(
-                out=codes[:, half * (w // 4) : (half + 1) * (w // 4)].bitcast(FP8X4),
-                scales=scales[:, half * (w // 4) : (half + 1) * (w // 4)],
-                in_=grouped[:, half * w : (half + 1) * w],
-            )
+            w = COLS // parts
+            for i in range(parts):
+                nc.vector.quantize_mx(
+                    out=codes[:, i * (w // 4) : (i + 1) * (w // 4)].bitcast(FP8X4),
+                    scales=scales[:, i * (w // 4) : (i + 1) * (w // 4)],
+                    in_=grouped[:, i * w : (i + 1) * w],
+                )
 
         def multiply(c):
             codes, scales = state[("q", c)]
@@ -138,15 +156,18 @@ def tile_samplinglayer_t_kernel(tc, x, weight, out):
                 o_sb = opool.tile([P, CH * K], F32)
                 state[("o", bt)] = o_sb
             o_sb = state[("o", bt)]
-            dst = o_sb[:, h * CH_CHUNK * K : (h + 1) * CH_CHUNK * K]
+            lo, hi = h * CH_CHUNK * K, (h + 1) * CH_CHUNK * K
             if c % 2 == 1:
-                nc.vector.tensor_copy(out=dst, in_=state[("ob", c)][:])
+                nc.vector.tensor_copy(out=o_sb[:, lo:hi], in_=state[("ob", c)][:])
             else:
-                nc.scalar.copy(out=dst, in_=state[("ob", c)][:])
-            if h == HALVES - 1:
-                nc.sync.dma_start(out=out[bt * P : (bt + 1) * P, :], in_=o_sb[:])
+                nc.scalar.copy(out=o_sb[:, lo:hi], in_=state[("ob", c)][:])
+            rows = out[bt * P : (bt + 1) * P, :]
+            if bt == N_BT - 1:
+                nc.sync.dma_start(out=rows[:, lo:hi], in_=o_sb[:, lo:hi])
+            elif h == HALVES - 1:
+                nc.sync.dma_start(out=rows, in_=o_sb[:])
 
-        for c in range(N_CHUNK + 1):
+        for c in range(N_CHUNK + 2):
             if c < N_CHUNK:
                 transposes(c)
                 grouped = gpool.tile([P, COLS], BF16, align_bytes=64)
@@ -154,13 +175,14 @@ def tile_samplinglayer_t_kernel(tc, x, weight, out):
                 codes = qpool.tile([P, COLS // 4], U32, align_bytes=64)
                 scales = qpool.tile([P, COLS // 4], U8, align_bytes=64)
                 state[("q", c)] = (codes, scales)
-                copy_bank(c, 0, "v")
-                copy_bank(c, 1, "s")
-                copy_bank(c, 2, "s")
-                copy_bank(c, 3, "s")
-                quantise(c, 0)
-            if c >= 1:
-                multiply(c - 1)
-                result(c - 1)
-            if c < N_CHUNK:
-                quantise(c, 1)
+                for p in range(CH_CHUNK):
+                    copy_bank(c, p, "v" if (p == 0 or (c == 0 and p < 3)) else "s")
+            if c == 0:
+                nc.vector.quantize_mx(
+                    out=w_codes[:].bitcast(FP8X4), scales=w_scales[:], in_=w_grouped[:]
+                )
+            if 1 <= c <= N_CHUNK:
+                quantise(c - 1, 2 if c == N_CHUNK else 1)
+            if c >= 2:
+                multiply(c - 2)
+                result(c - 2)

@@ -32,7 +32,7 @@ def tile_samplinglayer_t_kernel(tc, x, weight, out):
         fpool = ctx.enter_context(tc.tile_pool(name="fpool", bufs=CH_CHUNK))
         xpool = ctx.enter_context(tc.tile_pool(name="xpool", bufs=N_CHUNK - 1))
         gpool = ctx.enter_context(tc.tile_pool(name="gpool", bufs=3))
-        qpool = ctx.enter_context(tc.tile_pool(name="qpool", bufs=3))
+        qpool = ctx.enter_context(tc.tile_pool(name="qpool", bufs=4))
         opool = ctx.enter_context(tc.tile_pool(name="opool", bufs=N_BT))
         ps_t = ctx.enter_context(tc.psum_pool(name="ps_t", bufs=6))
         ps_o = ctx.enter_context(tc.psum_pool(name="ps_o", bufs=2))
@@ -108,7 +108,7 @@ def tile_samplinglayer_t_kernel(tc, x, weight, out):
                 if c == 0:
                     fillers(1)
             state[("xt", c)] = banks
-            if c < 2:
+            if c < 4:
                 fillers(FILL)
 
         def copy_bank(c, p, engine):
@@ -157,7 +157,7 @@ def tile_samplinglayer_t_kernel(tc, x, weight, out):
                 state[("o", bt)] = o_sb
             o_sb = state[("o", bt)]
             lo, hi = h * CH_CHUNK * K, (h + 1) * CH_CHUNK * K
-            if c % 2 == 1:
+            if c % 2 == 0 and bt < N_BT - 1:
                 nc.vector.tensor_copy(out=o_sb[:, lo:hi], in_=state[("ob", c)][:])
             else:
                 nc.scalar.copy(out=o_sb[:, lo:hi], in_=state[("ob", c)][:])
@@ -167,22 +167,31 @@ def tile_samplinglayer_t_kernel(tc, x, weight, out):
             elif h == HALVES - 1:
                 nc.sync.dma_start(out=rows, in_=o_sb[:])
 
-        for c in range(N_CHUNK + 2):
-            if c < N_CHUNK:
-                transposes(c)
-                grouped = gpool.tile([P, COLS], BF16, align_bytes=64)
-                state[("gr", c)] = grouped
-                codes = qpool.tile([P, COLS // 4], U32, align_bytes=64)
-                scales = qpool.tile([P, COLS // 4], U8, align_bytes=64)
-                state[("q", c)] = (codes, scales)
-                for p in range(CH_CHUNK):
-                    copy_bank(c, p, "v" if (p == 0 or (c == 0 and p < 3)) else "s")
-            if c == 0:
+        def front(c):
+            transposes(c)
+            grouped = gpool.tile([P, COLS], BF16, align_bytes=64)
+            state[("gr", c)] = grouped
+            codes = qpool.tile([P, COLS // 4], U32, align_bytes=64)
+            scales = qpool.tile([P, COLS // 4], U8, align_bytes=64)
+            state[("q", c)] = (codes, scales)
+            for p in range(CH_CHUNK):
+                copy_bank(c, p, "v" if (p == 0 or (c == 0 and p < 3)) else "s")
+
+        for i in range(N_BT + 1):
+            c0, c1 = 2 * i, 2 * i + 1
+            if i < N_BT:
+                front(c0)
+            if i == 0:
                 nc.vector.quantize_mx(
                     out=w_codes[:].bitcast(FP8X4), scales=w_scales[:], in_=w_grouped[:]
                 )
-            if 1 <= c <= N_CHUNK:
-                quantise(c - 1, 2 if c == N_CHUNK else 1)
-            if c >= 2:
-                multiply(c - 2)
-                result(c - 2)
+            if i >= 1:
+                quantise(c1 - 2, 2 if i == N_BT else 1)
+            if i < N_BT:
+                front(c1)
+                quantise(c0, 1)
+            if i >= 1:
+                multiply(c0 - 2)
+                multiply(c1 - 2)
+                result(c0 - 2)
+                result(c1 - 2)

@@ -40,7 +40,7 @@ def tile_samplinglayer_t_kernel(tc, x, weight, out):
 
         wz = const.tile([P, K], BF16)
         nc.vector.memset(wz[:], 0.0)
-        nc.sync.dma_start(out=wz[0:1, :], in_=weight.rearrange("(o k) -> o k", o=1))
+        nc.scalar.dma_start(out=wz[0:1, :], in_=weight.rearrange("(o k) -> o k", o=1))
         words = {}
         for p in range(CH_CHUNK):
             x_first = fpool.tile([P, L], BF16)
@@ -78,21 +78,23 @@ def tile_samplinglayer_t_kernel(tc, x, weight, out):
 
         fillers(WARM)
 
-        wb = ps_o.tile([P, K], F32, tag="ob")
-        nc.tensor.matmul(wb[:], lhsT=ones[:], rhs=wz[:], start=True, stop=True)
-        fillers(1)
-        sq = const.tile([P, 8, K], F32)
-        for j in range(8):
+        def make_w():
+            wb = ps_o.tile([P, K], F32, tag="ob")
+            nc.tensor.matmul(wb[:], lhsT=ones[:], rhs=wz[:], start=True, stop=True)
+            sq = const.tile([P, 8, K], F32)
+            for j in range(8):
+                nc.scalar.activation(
+                    out=sq[:, j, :], in_=wb[:], func=ACT.Square, bias=l_f32[:, j : j + 1], scale=-1.0
+                )
+            w_grouped = const.tile([P, PASSES * K * 4], BF16, align_bytes=64)
             nc.scalar.activation(
-                out=sq[:, j, :], in_=wb[:], func=ACT.Square, bias=l_f32[:, j : j + 1], scale=-1.0
+                out=w_grouped[:].rearrange("q (g k t) -> q g k t", g=PASSES, t=4),
+                in_=sq[:].rearrange("q (g t) k -> q g k t", g=PASSES),
+                func=ACT.Exp,
+                scale=-0.01,
             )
-        w_grouped = const.tile([P, PASSES * K * 4], BF16, align_bytes=64)
-        nc.scalar.activation(
-            out=w_grouped[:].rearrange("q (g k t) -> q g k t", g=PASSES, t=4),
-            in_=sq[:].rearrange("q (g t) k -> q g k t", g=PASSES),
-            func=ACT.Exp,
-            scale=-0.01,
-        )
+            return w_grouped
+
         w_codes = const.tile([P, PASSES * K], U32, align_bytes=64)
         w_scales = const.tile([P, PASSES * K], U8, align_bytes=64)
 
@@ -157,7 +159,7 @@ def tile_samplinglayer_t_kernel(tc, x, weight, out):
                 state[("o", bt)] = o_sb
             o_sb = state[("o", bt)]
             lo, hi = h * CH_CHUNK * K, (h + 1) * CH_CHUNK * K
-            if c % 2 == 0 and bt < N_BT - 1:
+            if c % 2 == 0 and 2 < bt < N_BT - 1 or c == 0:
                 nc.vector.tensor_copy(out=o_sb[:, lo:hi], in_=state[("ob", c)][:])
             else:
                 nc.scalar.copy(out=o_sb[:, lo:hi], in_=state[("ob", c)][:])
@@ -175,21 +177,23 @@ def tile_samplinglayer_t_kernel(tc, x, weight, out):
             scales = qpool.tile([P, COLS // 4], U8, align_bytes=64)
             state[("q", c)] = (codes, scales)
             for p in range(CH_CHUNK):
-                copy_bank(c, p, "v" if (p == 0 or (c == 0 and p < 3)) else "s")
+                copy_bank(c, p, "v" if (p == 0 or c == 0 or (c == 1 and p == 1)) else "s")
 
         for i in range(N_BT + 1):
             c0, c1 = 2 * i, 2 * i + 1
             if i < N_BT:
                 front(c0)
             if i == 0:
-                nc.vector.quantize_mx(
-                    out=w_codes[:].bitcast(FP8X4), scales=w_scales[:], in_=w_grouped[:]
-                )
+                w_grouped = make_w()
             if i >= 1:
                 quantise(c1 - 2, 2 if i == N_BT else 1)
             if i < N_BT:
                 front(c1)
                 quantise(c0, 1)
+            if i == 0:
+                nc.vector.quantize_mx(
+                    out=w_codes[:].bitcast(FP8X4), scales=w_scales[:], in_=w_grouped[:]
+                )
             if i >= 1:
                 multiply(c0 - 2)
                 multiply(c1 - 2)

@@ -21,8 +21,6 @@ HALVES = CH // CH_CHUNK
 N_CHUNK = N_BT * HALVES
 COLS = CH_CHUNK * L
 PASSES = L // 512
-WARM = 3
-FILL = 3
 
 
 def tile_samplinglayer_t_kernel(tc, x, weight, out):
@@ -70,14 +68,6 @@ def tile_samplinglayer_t_kernel(tc, x, weight, out):
         l_f32 = const.tile([P, 8], F32)
         nc.vector.tensor_copy(out=l_f32[:], in_=l_int[:])
 
-        idle = ps_o.tile([P, P], F32, tag="ob")
-
-        def fillers(n):
-            for i in range(n):
-                nc.tensor.matmul(idle[:], lhsT=ident[:], rhs=ident[:], start=True, stop=True)
-
-        fillers(WARM)
-
         def make_w():
             wb = ps_o.tile([P, K], F32, tag="ob")
             nc.tensor.matmul(wb[:], lhsT=ones[:], rhs=wz[:], start=True, stop=True)
@@ -107,11 +97,7 @@ def tile_samplinglayer_t_kernel(tc, x, weight, out):
                 for j in range(4):
                     nc.tensor.transpose(xt[:, j, :], words[(c, p)][:, j * P : (j + 1) * P], ident[:])
                 banks.append(xt)
-                if c == 0:
-                    fillers(1)
             state[("xt", c)] = banks
-            if c < 4:
-                fillers(FILL)
 
         def copy_bank(c, p, engine):
             grouped = state[("gr", c)]

@@ -38,12 +38,12 @@ def tile_samplinglayer_t_kernel(tc, x, weight, out):
 
         wz = const.tile([P, K], BF16)
         nc.vector.memset(wz[:], 0.0)
-        nc.scalar.dma_start(out=wz[0:1, :], in_=weight.rearrange("(o k) -> o k", o=1))
         words = {}
         for p in range(CH_CHUNK):
             x_first = fpool.tile([P, L], BF16)
             nc.sync.dma_start(out=x_first[:], in_=x[0:P, p * L : (p + 1) * L])
             words[(0, p)] = x_first[:].bitcast(F32)
+        nc.sync.dma_start(out=wz[0:1, :], in_=weight.rearrange("(o k) -> o k", o=1))
         for c in range(1, N_CHUNK):
             bt, h = divmod(c, HALVES)
             x_sb = xpool.tile([P, COLS], BF16)

@@ -18,8 +18,10 @@ FLOPS = 2 * B * CH * L * K
 CH_CHUNK = 4
 N_BT = B // P
 HALVES = CH // CH_CHUNK
+STORES = {0: 2, 2: 2, 4: 2, 6: 1, 7: 1}
 N_CHUNK = N_BT * HALVES
 COLS = CH_CHUNK * L
+FIRST = 2
 PASSES = L // 512
 
 
@@ -27,11 +29,11 @@ def tile_samplinglayer_t_kernel(tc, x, weight, out):
     nc = tc.nc
     with ExitStack() as ctx:
         const = ctx.enter_context(tc.tile_pool(name="const", bufs=1))
-        fpool = ctx.enter_context(tc.tile_pool(name="fpool", bufs=CH_CHUNK))
+        fpool = ctx.enter_context(tc.tile_pool(name="fpool", bufs=FIRST))
         xpool = ctx.enter_context(tc.tile_pool(name="xpool", bufs=N_CHUNK - 1))
         gpool = ctx.enter_context(tc.tile_pool(name="gpool", bufs=3))
         qpool = ctx.enter_context(tc.tile_pool(name="qpool", bufs=4))
-        opool = ctx.enter_context(tc.tile_pool(name="opool", bufs=N_BT))
+        opool = ctx.enter_context(tc.tile_pool(name="opool", bufs=len(STORES)))
         ps_t = ctx.enter_context(tc.psum_pool(name="ps_t", bufs=6))
         ps_o = ctx.enter_context(tc.psum_pool(name="ps_o", bufs=2))
         ctx.enter_context(tc.manual_schedule())
@@ -39,10 +41,14 @@ def tile_samplinglayer_t_kernel(tc, x, weight, out):
         wz = const.tile([P, K], BF16)
         nc.vector.memset(wz[:], 0.0)
         words = {}
-        for p in range(CH_CHUNK):
-            x_first = fpool.tile([P, L], BF16)
-            nc.sync.dma_start(out=x_first[:], in_=x[0:P, p * L : (p + 1) * L])
-            words[(0, p)] = x_first[:].bitcast(F32)
+        piece = COLS // FIRST
+        for i in range(FIRST):
+            x_first = fpool.tile([P, piece], BF16)
+            nc.sync.dma_start(out=x_first[:], in_=x[0:P, i * piece : (i + 1) * piece])
+            for j in range(CH_CHUNK // FIRST):
+                words[(0, i * (CH_CHUNK // FIRST) + j)] = x_first[:].bitcast(F32)[
+                    :, j * 512 : (j + 1) * 512
+                ]
         nc.sync.dma_start(out=wz[0:1, :], in_=weight.rearrange("(o k) -> o k", o=1))
         for c in range(1, N_CHUNK):
             bt, h = divmod(c, HALVES)
@@ -93,7 +99,7 @@ def tile_samplinglayer_t_kernel(tc, x, weight, out):
         def transposes(c):
             banks = []
             for p in range(CH_CHUNK):
-                xt = ps_t.tile([P, 4, P], F32)
+                xt = ps_t.tile([P, 4, P], F32, tag="xt")
                 for j in range(4):
                     nc.tensor.transpose(xt[:, j, :], words[(c, p)][:, j * P : (j + 1) * P], ident[:])
                 banks.append(xt)
@@ -110,25 +116,23 @@ def tile_samplinglayer_t_kernel(tc, x, weight, out):
             else:
                 nc.scalar.copy(out=dst, in_=src)
 
-        def quantise(c, parts):
+        def quantise(c, first=0, count=CH_CHUNK):
             grouped = state[("gr", c)]
             codes, scales = state[("q", c)]
-            w = COLS // parts
-            for i in range(parts):
-                nc.vector.quantize_mx(
-                    out=codes[:, i * (w // 4) : (i + 1) * (w // 4)].bitcast(FP8X4),
-                    scales=scales[:, i * (w // 4) : (i + 1) * (w // 4)],
-                    in_=grouped[:, i * w : (i + 1) * w],
-                )
+            lo, hi = first * L, (first + count) * L
+            nc.vector.quantize_mx(
+                out=codes[:, lo // 4 : hi // 4].bitcast(FP8X4),
+                scales=scales[:, lo // 4 : hi // 4],
+                in_=grouped[:, lo:hi],
+            )
 
-        def multiply(c):
+        def multiply(c, ob, first=0, count=CH_CHUNK):
             codes, scales = state[("q", c)]
-            ob = ps_o.tile([P, CH_CHUNK * K], F32, tag="ob")
-            for p in range(CH_CHUNK):
+            for p in range(first, first + count):
                 for g in range(PASSES):
                     col = (p * PASSES + g) * P
                     nc.tensor.matmul_mx(
-                        out=ob[:, p * K : (p + 1) * K],
+                        out=ob[:, (p - first) * K : (p - first + 1) * K],
                         lhsT=codes[:, col : col + P].bitcast(FP8X4),
                         lhsT_scale=scales[:, col : col + P],
                         rhs=w_codes[:, g * K : (g + 1) * K].bitcast(FP8X4),
@@ -136,24 +140,26 @@ def tile_samplinglayer_t_kernel(tc, x, weight, out):
                         start=(g == 0),
                         stop=(g == PASSES - 1),
                     )
-            state[("ob", c)] = ob
 
-        def result(c):
+        def result(c, ob, engine, first=0, count=CH_CHUNK):
             bt, h = divmod(c, HALVES)
-            if h == 0:
-                o_sb = opool.tile([P, CH * K], F32)
-                state[("o", bt)] = o_sb
-            o_sb = state[("o", bt)]
-            lo, hi = h * CH_CHUNK * K, (h + 1) * CH_CHUNK * K
-            if c % 2 == 0 and 2 < bt < N_BT - 1 or c == 0:
-                nc.vector.tensor_copy(out=o_sb[:, lo:hi], in_=state[("ob", c)][:])
+            if h == 0 and first == 0 and bt in STORES:
+                o_sb = opool.tile([P, STORES[bt], CH * K], F32)
+                for t in range(STORES[bt]):
+                    state[("o", bt + t)] = o_sb[:, t, :]
+                state[("os", bt)] = o_sb
+            lo = (h * CH_CHUNK + first) * K
+            dst = state[("o", bt)][:, lo : lo + count * K]
+            if engine == "v":
+                nc.vector.tensor_copy(out=dst, in_=ob[:, : count * K])
             else:
-                nc.scalar.copy(out=o_sb[:, lo:hi], in_=state[("ob", c)][:])
-            rows = out[bt * P : (bt + 1) * P, :]
-            if bt == N_BT - 1:
-                nc.sync.dma_start(out=rows[:, lo:hi], in_=o_sb[:, lo:hi])
-            elif h == HALVES - 1:
-                nc.sync.dma_start(out=rows, in_=o_sb[:])
+                nc.scalar.copy(out=dst, in_=ob[:, : count * K])
+
+        def store(bt):
+            for b0, n in STORES.items():
+                if b0 + n - 1 == bt:
+                    rows = out[b0 * P : (bt + 1) * P, :].rearrange("(t q) c -> q t c", t=n)
+                    nc.sync.dma_start(out=rows, in_=state[("os", b0)][:])
 
         def front(c):
             transposes(c)
@@ -165,23 +171,38 @@ def tile_samplinglayer_t_kernel(tc, x, weight, out):
             for p in range(CH_CHUNK):
                 copy_bank(c, p, "v" if (p == 0 or c == 0 or (c == 1 and p == 1)) else "s")
 
-        for i in range(N_BT + 1):
+        for i in range(N_BT):
             c0, c1 = 2 * i, 2 * i + 1
-            if i < N_BT:
-                front(c0)
+            front(c0)
             if i == 0:
                 w_grouped = make_w()
-            if i >= 1:
-                quantise(c1 - 2, 2 if i == N_BT else 1)
-            if i < N_BT:
-                front(c1)
-                quantise(c0, 1)
+            else:
+                quantise(c0 - 1)
+            front(c1)
+            quantise(c0)
             if i == 0:
                 nc.vector.quantize_mx(
                     out=w_codes[:].bitcast(FP8X4), scales=w_scales[:], in_=w_grouped[:]
                 )
-            if i >= 1:
-                multiply(c0 - 2)
-                multiply(c1 - 2)
-                result(c0 - 2)
-                result(c1 - 2)
+            else:
+                obs = []
+                for c in (c0 - 2, c0 - 1):
+                    ob = ps_o.tile([P, CH_CHUNK * K], F32, tag="ob")
+                    multiply(c, ob)
+                    obs.append(ob)
+                result(c0 - 2, obs[0], "v" if i == 1 or 4 <= i < N_BT - 1 else "s")
+                result(c0 - 1, obs[1], "s")
+                store(i - 1)
+
+        c0, c1 = N_CHUNK - 2, N_CHUNK - 1
+        ob = ps_t.tile([P, CH_CHUNK * K], F32, tag="xt")
+        multiply(c0, ob)
+        result(c0, ob, "s")
+        half = CH_CHUNK // 2
+        for first in range(0, CH_CHUNK, half):
+            ob = ps_t.tile([P, half * K], F32, tag="xt")
+            for p in range(first, first + half):
+                quantise(c1, p, 1)
+            multiply(c1, ob, first, half)
+            result(c1, ob, "v" if first else "s", first, half)
+        store(N_BT - 1)

from contextlib import ExitStack

import concourse.mybir as mybir
from concourse.masks import make_identity

F32 = mybir.dt.float32
BF16 = mybir.dt.bfloat16
U32 = mybir.dt.uint32
U8 = mybir.dt.uint8
I32 = mybir.dt.int32
FP8X4 = mybir.dt.float8_e4m3fn_x4
ACT = mybir.ActivationFunctionType

P = 128
B, CH, L, K = 1024, 8, 1024, 128
FLOPS = 2 * B * CH * L * K

CH_CHUNK = 4
N_BT = B // P
HALVES = CH // CH_CHUNK
STORES = {0: 2, 2: 2, 4: 2, 6: 1, 7: 1}
N_CHUNK = N_BT * HALVES
COLS = CH_CHUNK * L
FIRST = 2
PASSES = L // 512


def tile_samplinglayer_t_kernel(tc, x, weight, out):
    nc = tc.nc
    with ExitStack() as ctx:
        const = ctx.enter_context(tc.tile_pool(name="const", bufs=1))
        fpool = ctx.enter_context(tc.tile_pool(name="fpool", bufs=FIRST))
        xpool = ctx.enter_context(tc.tile_pool(name="xpool", bufs=N_CHUNK - 1))
        gpool = ctx.enter_context(tc.tile_pool(name="gpool", bufs=3))
        qpool = ctx.enter_context(tc.tile_pool(name="qpool", bufs=4))
        opool = ctx.enter_context(tc.tile_pool(name="opool", bufs=len(STORES)))
        ps_t = ctx.enter_context(tc.psum_pool(name="ps_t", bufs=6))
        ps_o = ctx.enter_context(tc.psum_pool(name="ps_o", bufs=2))
        ctx.enter_context(tc.manual_schedule())

        wz = const.tile([P, K], BF16)
        nc.vector.memset(wz[:], 0.0)
        words = {}
        piece = COLS // FIRST
        for i in range(FIRST):
            x_first = fpool.tile([P, piece], BF16)
            nc.sync.dma_start(out=x_first[:], in_=x[0:P, i * piece : (i + 1) * piece])
            for j in range(CH_CHUNK // FIRST):
                words[(0, i * (CH_CHUNK // FIRST) + j)] = x_first[:].bitcast(F32)[
                    :, j * 512 : (j + 1) * 512
                ]
        nc.sync.dma_start(out=wz[0:1, :], in_=weight.rearrange("(o k) -> o k", o=1))
        for c in range(1, N_CHUNK):
            bt, h = divmod(c, HALVES)
            x_sb = xpool.tile([P, COLS], BF16)
            nc.sync.dma_start(
                out=x_sb[:], in_=x[bt * P : (bt + 1) * P, h * COLS : (h + 1) * COLS]
            )
            for p in range(CH_CHUNK):
                words[(c, p)] = x_sb[:].bitcast(F32)[:, p * 512 : (p + 1) * 512]

        ident = const.tile([P, P], F32)
        make_identity(nc, ident[:])
        ones = const.tile([P, P], BF16)
        nc.vector.memset(ones[:], 1.0)
        tiny = const.tile([P, 1], F32)
        nc.vector.memset(tiny[:], 0.0)
        tiny2 = const.tile([P, 1], F32)
        nc.scalar.activation(out=tiny2[:], in_=tiny[:], func=ACT.Exp)
        l_int = const.tile([P, 8], I32)
        nc.gpsimd.iota(
            l_int[:], pattern=[[512, 2], [256, 2], [1, 2]], base=1, channel_multiplier=2
        )
        l_f32 = const.tile([P, 8], F32)
        nc.vector.tensor_copy(out=l_f32[:], in_=l_int[:])

        def make_w():
            wb = ps_o.tile([P, K], F32, tag="ob")
            nc.tensor.matmul(wb[:], lhsT=ones[:], rhs=wz[:], start=True, stop=True)
            sq = const.tile([P, 8, K], F32)
            for j in range(8):
                nc.scalar.activation(
                    out=sq[:, j, :], in_=wb[:], func=ACT.Square, bias=l_f32[:, j : j + 1], scale=-1.0
                )
            w_grouped = const.tile([P, PASSES * K * 4], BF16, align_bytes=64)
            nc.scalar.activation(
                out=w_grouped[:].rearrange("q (g k t) -> q g k t", g=PASSES, t=4),
                in_=sq[:].rearrange("q (g t) k -> q g k t", g=PASSES),
                func=ACT.Exp,
                scale=-0.01,
            )
            return w_grouped

        w_codes = const.tile([P, PASSES * K], U32, align_bytes=64)
        w_scales = const.tile([P, PASSES * K], U8, align_bytes=64)

        state = {}

        def transposes(c):
            banks = []
            for p in range(CH_CHUNK):
                xt = ps_t.tile([P, 4, P], F32, tag="xt")
                for j in range(4):
                    nc.tensor.transpose(xt[:, j, :], words[(c, p)][:, j * P : (j + 1) * P], ident[:])
                banks.append(xt)
            state[("xt", c)] = banks

        def copy_bank(c, p, engine):
            grouped = state[("gr", c)]
            dst = grouped[:].bitcast(F32)[:, p * 512 : (p + 1) * 512].rearrange(
                "q (g b u) -> q g b u", g=PASSES, u=2
            )
            src = state[("xt", c)][p][:].rearrange("q (g u) b -> q g b u", u=2)
            if engine == "v":
                nc.vector.tensor_copy(out=dst, in_=src)
            else:
                nc.scalar.copy(out=dst, in_=src)

        def quantise(c, first=0, count=CH_CHUNK):
            grouped = state[("gr", c)]
            codes, scales = state[("q", c)]
            lo, hi = first * L, (first + count) * L
            nc.vector.quantize_mx(
                out=codes[:, lo // 4 : hi // 4].bitcast(FP8X4),
                scales=scales[:, lo // 4 : hi // 4],
                in_=grouped[:, lo:hi],
            )

        def multiply(c, ob, first=0, count=CH_CHUNK):
            codes, scales = state[("q", c)]
            for p in range(first, first + count):
                for g in range(PASSES):
                    col = (p * PASSES + g) * P
                    nc.tensor.matmul_mx(
                        out=ob[:, (p - first) * K : (p - first + 1) * K],
                        lhsT=codes[:, col : col + P].bitcast(FP8X4),
                        lhsT_scale=scales[:, col : col + P],
                        rhs=w_codes[:, g * K : (g + 1) * K].bitcast(FP8X4),
                        rhs_scale=w_scales[:, g * K : (g + 1) * K],
                        start=(g == 0),
                        stop=(g == PASSES - 1),
                    )

        def result(c, ob, engine, first=0, count=CH_CHUNK):
            bt, h = divmod(c, HALVES)
            if h == 0 and first == 0 and bt in STORES:
                o_sb = opool.tile([P, STORES[bt], CH * K], F32)
                for t in range(STORES[bt]):
                    state[("o", bt + t)] = o_sb[:, t, :]
                state[("os", bt)] = o_sb
            lo = (h * CH_CHUNK + first) * K
            dst = state[("o", bt)][:, lo : lo + count * K]
            if engine == "v":
                nc.vector.tensor_copy(out=dst, in_=ob[:, : count * K])
            else:
                nc.scalar.copy(out=dst, in_=ob[:, : count * K])

        def store(bt):
            for b0, n in STORES.items():
                if b0 + n - 1 == bt:
                    rows = out[b0 * P : (bt + 1) * P, :].rearrange("(t q) c -> q t c", t=n)
                    nc.sync.dma_start(out=rows, in_=state[("os", b0)][:])

        def front(c):
            transposes(c)
            grouped = gpool.tile([P, COLS], BF16, align_bytes=64)
            state[("gr", c)] = grouped
            codes = qpool.tile([P, COLS // 4], U32, align_bytes=64)
            scales = qpool.tile([P, COLS // 4], U8, align_bytes=64)
            state[("q", c)] = (codes, scales)
            for p in range(CH_CHUNK):
                copy_bank(c, p, "v" if (p == 0 or c == 0 or (c == 1 and p == 1)) else "s")

        for i in range(N_BT):
            c0, c1 = 2 * i, 2 * i + 1
            front(c0)
            if i == 0:
                w_grouped = make_w()
            else:
                quantise(c0 - 1)
            front(c1)
            quantise(c0)
            if i == 0:
                nc.vector.quantize_mx(
                    out=w_codes[:].bitcast(FP8X4), scales=w_scales[:], in_=w_grouped[:]
                )
            else:
                obs = []
                for c in (c0 - 2, c0 - 1):
                    ob = ps_o.tile([P, CH_CHUNK * K], F32, tag="ob")
                    multiply(c, ob)
                    obs.append(ob)
                result(c0 - 2, obs[0], "v" if i == 1 or 4 <= i < N_BT - 1 else "s")
                result(c0 - 1, obs[1], "s")
                store(i - 1)

        c0, c1 = N_CHUNK - 2, N_CHUNK - 1
        ob = ps_t.tile([P, CH_CHUNK * K], F32, tag="xt")
        multiply(c0, ob)
        result(c0, ob, "s")
        half = CH_CHUNK // 2
        for first in range(0, CH_CHUNK, half):
            ob = ps_t.tile([P, half * K], F32, tag="xt")
            for p in range(first, first + half):
                quantise(c1, p, 1)
            multiply(c1, ob, first, half)
            result(c1, ob, "v" if first else "s", first, half)
        store(N_BT - 1)
